import numpy as np
import ml_dtypes


def mxq(x, axis, fmt="e4m3"):
    dtype, down = {"e4m3": (ml_dtypes.float8_e4m3fn, 7), "e5m2": (ml_dtypes.float8_e5m2, 14)}[fmt]
    v = np.moveaxis(np.asarray(x, np.float32).astype(ml_dtypes.bfloat16).astype(np.float64), axis, -1)
    blocks = v.reshape(v.shape[:-1] + (-1, 32))
    amax = np.abs(blocks).max(-1, keepdims=True)
    byte = np.maximum(np.where(amax > 0, np.frexp(amax)[1] - 1 + 127, 0) - down, 1)
    scale = np.exp2(byte - 127.0)
    codes = (blocks / scale).astype(np.float32).astype(dtype).astype(np.float64)
    return np.moveaxis((codes * scale).reshape(v.shape), -1, axis)


WIDE = False


def mx_kscale(k, group=512):
    if not WIDE:
        return np.ones(k)
    levels = np.array([10, -10, 5, -5, 0])
    if group != 512:
        return np.exp2(np.random.permutation(np.resize(levels, k // group))).repeat(group)
    a = np.random.permutation(np.resize(levels, k // 512 * 4)).reshape(k // 512, 4)
    idx = np.arange(k)
    return np.exp2(a[idx // 512, idx % 128 // 32])


BF16 = ml_dtypes.bfloat16


def bf(x):
    return np.asarray(x, np.float32).astype(BF16)


def f64(x):
    return np.asarray(x).astype(np.float64)


B, T, D, F = 2, 32, 8192, 4096
TRIPLES = [(1, 2, 3), (1, 4, 5), (1, 7, 6), (2, 4, 6), (2, 5, 7), (3, 4, 7), (3, 6, 5)]
O = len(TRIPLES) + 1
D8, F8 = D // O, F // O


def oct_table():
    tab = [[None] * O for _ in range(O)]
    tab[0][0] = (0, 1.0)
    for i in range(1, O):
        tab[i][i] = (0, 1.0)
        tab[0][i] = (i, 1.0)
        tab[i][0] = (i, -1.0)
    for a, b, c in TRIPLES:
        for p, q, r in ((a, b, c), (b, c, a), (c, a, b)):
            tab[q][r] = (p, 1.0)
            tab[p][r] = (q, -1.0)
    return tab


def oct_linear(xq, w):
    tab = oct_table()
    p = (xq @ mxq(w.reshape(F, D8).T, 0, "e4m3")).reshape(B, T, O, O, F8)
    return np.concatenate([sum(tab[i][k][1] * p[:, :, i, tab[i][k][0]] for i in range(O)) for k in range(O)], axis=2)


def silu(v):
    return v / (1.0 + np.exp(-v))


def setup_inputs():
    s8 = mx_kscale(D8, D8 // 2)
    return {"x": bf(np.random.standard_normal((B, T, D)) * np.tile(s8, O)),
            "wq_gate": bf(np.random.standard_normal((O, F8, D8)) / np.sqrt(D) / s8),
            "wq_up": bf(np.random.standard_normal((O, F8, D8)) / np.sqrt(D) / s8)}


def reference(x, wq_gate, wq_up):
    xq = mxq(f64(x).reshape(B, T, O, D8), 3, "e4m3")
    gate = oct_linear(xq, f64(wq_gate))
    up = oct_linear(xq, f64(wq_up))
    return silu(gate) * up

@@ -1,0 +1,201 @@
+from contextlib import ExitStack
+
+import concourse.mybir as mybir
+from concourse.masks import make_identity
+
+F32 = mybir.dt.float32
+BF16 = mybir.dt.bfloat16
+U32 = mybir.dt.uint32
+U8 = mybir.dt.uint8
+FP8X4 = mybir.dt.float8_e4m3fn_x4
+
+P = 128
+PACK = 4
+K_PASS = P * PACK
+TRIPLES = [(1, 2, 3), (1, 4, 5), (1, 7, 6), (2, 4, 6), (2, 5, 7), (3, 4, 7), (3, 6, 5)]
+O = 8
+ROWS = 64
+D8 = 1024
+F8 = 512
+PASSES = D8 // K_PASS
+PAIRS = O // 2
+CHUNKS = F8 // P
+WORD_BLOCKS = D8 // 2 // P
+BLOCKS_AHEAD = 8
+
+FLOPS = 2 * 2 * ROWS * O * O * F8 * D8
+
+
+def octonion_sources():
+    source = {(0, 0): (0, 1.0)}
+    for i in range(1, O):
+        source[(0, i)] = (i, 1.0)
+        source[(i, i)] = (0, 1.0)
+        source[(i, 0)] = (i, -1.0)
+    for a, b, c in TRIPLES:
+        for p, q, r in ((a, b, c), (b, c, a), (c, a, b)):
+            source[(p, r)] = (q, 1.0)
+            source[(q, r)] = (p, -1.0)
+    return source
+
+
+def tile_swiglumlp_pa_kernel(tc, x, wq_gate, wq_up, out):
+    nc = tc.nc
+    source = octonion_sources()
+
+    x_halves = x.rearrange("b t (h f) -> (b t h) f", h=2)
+    blocks = [[x_halves[:, l * D8 : (l + 1) * D8] for l in range(CHUNKS)]]
+    for w in (wq_gate, wq_up):
+        for j in range(O):
+            blocks.append([w[j, c * P : (c + 1) * P, :] for c in range(CHUNKS)])
+    out_parts = out.rearrange("b t (k o) -> k (b t) o", o=F8)
+
+    with ExitStack() as ctx:
+        keep = ctx.enter_context(tc.tile_pool(name="keep", bufs=1))
+        raw_pool = ctx.enter_context(tc.tile_pool(name="raw", bufs=BLOCKS_AHEAD * CHUNKS))
+        grouped_pool = ctx.enter_context(tc.tile_pool(name="grouped", bufs=2))
+        w_mx_pool = ctx.enter_context(tc.tile_pool(name="w_mx", bufs=2))
+        result_pool = ctx.enter_context(tc.tile_pool(name="result", bufs=PAIRS))
+        flipped_pool = ctx.enter_context(tc.psum_pool(name="flipped", bufs=4))
+        acc_pool = ctx.enter_context(tc.psum_pool(name="acc", bufs=1))
+        ctx.enter_context(tc.manual_schedule())
+
+        raw = {}
+
+        def load_block(b):
+            raw[b] = []
+            for c in range(CHUNKS):
+                chunk = raw_pool.tile([P, D8], BF16, name="chunk")
+                nc.sync.dma_start(out=chunk[:], in_=blocks[b][c])
+                raw[b].append(chunk)
+
+        for b in range(BLOCKS_AHEAD):
+            load_block(b)
+
+        identity = keep.tile([P, P], F32, name="identity")
+        make_identity(nc, identity[:])
+
+        warm = keep.tile([P, 1], F32, name="warm")
+        nc.vector.memset(warm[:], 0.0)
+        nc.scalar.activation(out=warm[:], in_=warm[:], func=mybir.ActivationFunctionType.Silu)
+
+        def transpose_chunk(b, c):
+            words = raw[b][c][:].bitcast(F32)
+            flipped = flipped_pool.tile([P, WORD_BLOCKS, P], F32, name="flipped")
+            for s in range(WORD_BLOCKS):
+                nc.tensor.transpose(flipped[:, s, :], words[:, s * P : (s + 1) * P], identity[:])
+            return flipped
+
+        x_signed = keep.tile([P, 2, O, PASSES, ROWS * PACK], BF16, name="x_signed", align_bytes=64)
+        for l in range(CHUNKS):
+            flipped = transpose_chunk(0, l)
+            by_half = flipped[:].rearrange("p (g u) (r h) -> p h g r u", u=2, h=2)
+            for h in range(2):
+                words_out = x_signed[:, 0, 4 * h + l].bitcast(F32).rearrange(
+                    "p g (r u) -> p g r u", u=2
+                )
+                if l % 2 == 0:
+                    nc.vector.tensor_copy(out=words_out, in_=by_half[:, h])
+                else:
+                    nc.scalar.copy(out=words_out, in_=by_half[:, h])
+        load_block(BLOCKS_AHEAD)
+
+        x_codes = [
+            keep.tile([P, PAIRS, PASSES, P], U32, name="x_codes%d" % j, align_bytes=64)
+            for j in range(O)
+        ]
+        x_scales = [
+            keep.tile([P, PAIRS, PASSES, P], U8, name="x_scales%d" % j, align_bytes=64)
+            for j in range(O)
+        ]
+
+        def quantise_x_for(j):
+            for pair in range(PAIRS):
+                for half in range(2):
+                    i, sign = source[(j, 2 * pair + half)]
+                    columns = slice(half * ROWS, (half + 1) * ROWS)
+                    for g in range(PASSES):
+                        nc.vector.quantize_mx(
+                            out=x_codes[j][:, pair, g, columns].bitcast(FP8X4),
+                            scales=x_scales[j][:, pair, g, columns],
+                            in_=x_signed[:, 0 if sign > 0 else 1, i, g, :],
+                        )
+
+        w_mx = {}
+
+        def prepare_w(n):
+            grouped = grouped_pool.tile([P, PASSES, F8 * PACK], BF16, name="grouped", align_bytes=64)
+            grouped_words = grouped[:].bitcast(F32).rearrange("p g (o u) -> p g o u", u=2)
+            for c in range(CHUNKS):
+                flipped = transpose_chunk(n + 1, c)
+                nc.scalar.copy(
+                    out=grouped_words[:, :, c * P : (c + 1) * P, :],
+                    in_=flipped[:].rearrange("p (g u) o -> p g o u", u=2),
+                )
+            if n + 1 + BLOCKS_AHEAD < len(blocks):
+                load_block(n + 1 + BLOCKS_AHEAD)
+            return grouped
+
+        def quantise_w(n, grouped):
+            codes = w_mx_pool.tile([P, PASSES, F8], U32, name="w_codes", align_bytes=64)
+            scales = w_mx_pool.tile([P, PASSES, F8], U8, name="w_scales", align_bytes=64)
+            nc.vector.quantize_mx(
+                out=codes[:].rearrange("p g o -> p (g o)").bitcast(FP8X4),
+                scales=scales[:].rearrange("p g o -> p (g o)"),
+                in_=grouped[:].rearrange("p g c -> p (g c)"),
+            )
+            w_mx[n] = (codes, scales)
+
+        acc = {}
+        gate_act = {}
+
+        def multiply(n):
+            j = n % O
+            codes, scales = w_mx[n]
+            for pair in range(PAIRS):
+                if j == 0:
+                    acc[pair] = acc_pool.tile([P, F8], F32, name="acc%d" % pair)
+                for g in range(PASSES):
+                    nc.tensor.matmul_mx(
+                        out=acc[pair][:],
+                        lhsT=x_codes[j][:, pair, g, :].bitcast(FP8X4),
+                        lhsT_scale=x_scales[j][:, pair, g, :],
+                        rhs=codes[:, g, :].bitcast(FP8X4),
+                        rhs_scale=scales[:, g, :],
+                        start=(j == 0 and g == 0),
+                        stop=(j == O - 1 and g == PASSES - 1),
+                    )
+                if n == O - 1:
+                    gate_act[pair] = keep.tile([P, F8], F32, name="gate_act%d" % pair)
+                    nc.scalar.activation(
+                        out=gate_act[pair][:],
+                        in_=acc[pair][:],
+                        func=mybir.ActivationFunctionType.Silu,
+                    )
+                if n == 2 * O - 1:
+                    result = result_pool.tile([P, F8], F32, name="result")
+                    nc.vector.tensor_tensor(
+                        out=result[:], in0=acc[pair][:], in1=gate_act[pair][:], op=mybir.AluOpType.mult
+                    )
+                    for half in range(2):
+                        nc.sync.dma_start(
+                            out=out_parts[2 * pair + half],
+                            in_=result[half * ROWS : (half + 1) * ROWS, :],
+                        )
+
+        quantise_x_for(0)
+        quantise_w(0, prepare_w(0))
+        nc.vector.tensor_scalar(
+            out=x_signed[:, 1].rearrange("p i g c -> p (i g c)"),
+            in0=x_signed[:, 0].rearrange("p i g c -> p (i g c)"),
+            scalar1=-1.0,
+            scalar2=None,
+            op0=mybir.AluOpType.mult,
+        )
+        for n in range(2 * O):
+            if n + 1 < 2 * O:
+                grouped = prepare_w(n + 1)
+                if n + 1 < O:
+                    quantise_x_for(n + 1)
+                quantise_w(n + 1, grouped)
+            multiply(n)

@@ -22,6 +22,7 @@ PAIRS = O // 2
 CHUNKS = F8 // P
 WORD_BLOCKS = D8 // 2 // P
 BLOCKS_AHEAD = 8
+RUN = 2
 
 FLOPS = 2 * 2 * ROWS * O * O * F8 * D8
 
@@ -54,7 +55,7 @@ def tile_swiglumlp_pa_kernel(tc, x, wq_gate, wq_up, out):
         keep = ctx.enter_context(tc.tile_pool(name="keep", bufs=1))
         raw_pool = ctx.enter_context(tc.tile_pool(name="raw", bufs=BLOCKS_AHEAD * CHUNKS))
         grouped_pool = ctx.enter_context(tc.tile_pool(name="grouped", bufs=2))
-        w_mx_pool = ctx.enter_context(tc.tile_pool(name="w_mx", bufs=2))
+        w_mx_pool = ctx.enter_context(tc.tile_pool(name="w_mx", bufs=RUN + 1))
         result_pool = ctx.enter_context(tc.tile_pool(name="result", bufs=PAIRS))
         flipped_pool = ctx.enter_context(tc.psum_pool(name="flipped", bufs=4))
         acc_pool = ctx.enter_context(tc.psum_pool(name="acc", bufs=1))
@@ -128,15 +129,13 @@ def tile_swiglumlp_pa_kernel(tc, x, wq_gate, wq_up, out):
             grouped_words = grouped[:].bitcast(F32).rearrange("p g (o u) -> p g o u", u=2)
             for c in range(CHUNKS):
                 flipped = transpose_chunk(n + 1, c)
-                nc.scalar.copy(
+                copy_out = nc.vector.tensor_copy if c == CHUNKS - 1 else nc.scalar.copy
+                copy_out(
                     out=grouped_words[:, :, c * P : (c + 1) * P, :],
                     in_=flipped[:].rearrange("p (g u) o -> p g o u", u=2),
                 )
             if n + 1 + BLOCKS_AHEAD < len(blocks):
                 load_block(n + 1 + BLOCKS_AHEAD)
-            return grouped
-
-        def quantise_w(n, grouped):
             codes = w_mx_pool.tile([P, PASSES, F8], U32, name="w_codes", align_bytes=64)
             scales = w_mx_pool.tile([P, PASSES, F8], U8, name="w_scales", align_bytes=64)
             nc.vector.quantize_mx(
@@ -184,7 +183,7 @@ def tile_swiglumlp_pa_kernel(tc, x, wq_gate, wq_up, out):
                         )
 
         quantise_x_for(0)
-        quantise_w(0, prepare_w(0))
+        prepare_w(0)
         nc.vector.tensor_scalar(
             out=x_signed[:, 1].rearrange("p i g c -> p (i g c)"),
             in0=x_signed[:, 0].rearrange("p i g c -> p (i g c)"),
@@ -192,10 +191,13 @@ def tile_swiglumlp_pa_kernel(tc, x, wq_gate, wq_up, out):
             scalar2=None,
             op0=mybir.AluOpType.mult,
         )
+        for n in range(1, RUN):
+            quantise_x_for(n)
+            prepare_w(n)
         for n in range(2 * O):
-            if n + 1 < 2 * O:
-                grouped = prepare_w(n + 1)
-                if n + 1 < O:
-                    quantise_x_for(n + 1)
-                quantise_w(n + 1, grouped)
+            if n % RUN == RUN - 1:
+                for ahead in range(n + 1, min(n + 1 + RUN, 2 * O)):
+                    if ahead < O:
+                        quantise_x_for(ahead)
+                    prepare_w(ahead)
             multiply(n)

@@ -22,7 +22,7 @@ PAIRS = O // 2
 CHUNKS = F8 // P
 WORD_BLOCKS = D8 // 2 // P
 BLOCKS_AHEAD = 8
-RUN = 2
+RUN = 1
 
 FLOPS = 2 * 2 * ROWS * O * O * F8 * D8
 

from contextlib import ExitStack

import concourse.mybir as mybir
from concourse.masks import make_identity

F32 = mybir.dt.float32
BF16 = mybir.dt.bfloat16
U32 = mybir.dt.uint32
U8 = mybir.dt.uint8
FP8X4 = mybir.dt.float8_e4m3fn_x4

P = 128
PACK = 4
K_PASS = P * PACK
TRIPLES = [(1, 2, 3), (1, 4, 5), (1, 7, 6), (2, 4, 6), (2, 5, 7), (3, 4, 7), (3, 6, 5)]
O = 8
ROWS = 64
D8 = 1024
F8 = 512
PASSES = D8 // K_PASS
PAIRS = O // 2
CHUNKS = F8 // P
WORD_BLOCKS = D8 // 2 // P
BLOCKS_AHEAD = 8
RUN = 1

FLOPS = 2 * 2 * ROWS * O * O * F8 * D8


def octonion_sources():
    source = {(0, 0): (0, 1.0)}
    for i in range(1, O):
        source[(0, i)] = (i, 1.0)
        source[(i, i)] = (0, 1.0)
        source[(i, 0)] = (i, -1.0)
    for a, b, c in TRIPLES:
        for p, q, r in ((a, b, c), (b, c, a), (c, a, b)):
            source[(p, r)] = (q, 1.0)
            source[(q, r)] = (p, -1.0)
    return source


def tile_swiglumlp_pa_kernel(tc, x, wq_gate, wq_up, out):
    nc = tc.nc
    source = octonion_sources()

    x_halves = x.rearrange("b t (h f) -> (b t h) f", h=2)
    blocks = [[x_halves[:, l * D8 : (l + 1) * D8] for l in range(CHUNKS)]]
    for w in (wq_gate, wq_up):
        for j in range(O):
            blocks.append([w[j, c * P : (c + 1) * P, :] for c in range(CHUNKS)])
    out_parts = out.rearrange("b t (k o) -> k (b t) o", o=F8)

    with ExitStack() as ctx:
        keep = ctx.enter_context(tc.tile_pool(name="keep", bufs=1))
        raw_pool = ctx.enter_context(tc.tile_pool(name="raw", bufs=BLOCKS_AHEAD * CHUNKS))
        grouped_pool = ctx.enter_context(tc.tile_pool(name="grouped", bufs=2))
        w_mx_pool = ctx.enter_context(tc.tile_pool(name="w_mx", bufs=RUN + 1))
        result_pool = ctx.enter_context(tc.tile_pool(name="result", bufs=PAIRS))
        flipped_pool = ctx.enter_context(tc.psum_pool(name="flipped", bufs=4))
        acc_pool = ctx.enter_context(tc.psum_pool(name="acc", bufs=1))
        ctx.enter_context(tc.manual_schedule())

        raw = {}

        def load_block(b):
            raw[b] = []
            for c in range(CHUNKS):
                chunk = raw_pool.tile([P, D8], BF16, name="chunk")
                nc.sync.dma_start(out=chunk[:], in_=blocks[b][c])
                raw[b].append(chunk)

        for b in range(BLOCKS_AHEAD):
            load_block(b)

        identity = keep.tile([P, P], F32, name="identity")
        make_identity(nc, identity[:])

        warm = keep.tile([P, 1], F32, name="warm")
        nc.vector.memset(warm[:], 0.0)
        nc.scalar.activation(out=warm[:], in_=warm[:], func=mybir.ActivationFunctionType.Silu)

        def transpose_chunk(b, c):
            words = raw[b][c][:].bitcast(F32)
            flipped = flipped_pool.tile([P, WORD_BLOCKS, P], F32, name="flipped")
            for s in range(WORD_BLOCKS):
                nc.tensor.transpose(flipped[:, s, :], words[:, s * P : (s + 1) * P], identity[:])
            return flipped

        x_signed = keep.tile([P, 2, O, PASSES, ROWS * PACK], BF16, name="x_signed", align_bytes=64)
        for l in range(CHUNKS):
            flipped = transpose_chunk(0, l)
            by_half = flipped[:].rearrange("p (g u) (r h) -> p h g r u", u=2, h=2)
            for h in range(2):
                words_out = x_signed[:, 0, 4 * h + l].bitcast(F32).rearrange(
                    "p g (r u) -> p g r u", u=2
                )
                if l % 2 == 0:
                    nc.vector.tensor_copy(out=words_out, in_=by_half[:, h])
                else:
                    nc.scalar.copy(out=words_out, in_=by_half[:, h])
        load_block(BLOCKS_AHEAD)

        x_codes = [
            keep.tile([P, PAIRS, PASSES, P], U32, name="x_codes%d" % j, align_bytes=64)
            for j in range(O)
        ]
        x_scales = [
            keep.tile([P, PAIRS, PASSES, P], U8, name="x_scales%d" % j, align_bytes=64)
            for j in range(O)
        ]

        def quantise_x_for(j):
            for pair in range(PAIRS):
                for half in range(2):
                    i, sign = source[(j, 2 * pair + half)]
                    columns = slice(half * ROWS, (half + 1) * ROWS)
                    for g in range(PASSES):
                        nc.vector.quantize_mx(
                            out=x_codes[j][:, pair, g, columns].bitcast(FP8X4),
                            scales=x_scales[j][:, pair, g, columns],
                            in_=x_signed[:, 0 if sign > 0 else 1, i, g, :],
                        )

        w_mx = {}

        def prepare_w(n):
            grouped = grouped_pool.tile([P, PASSES, F8 * PACK], BF16, name="grouped", align_bytes=64)
            grouped_words = grouped[:].bitcast(F32).rearrange("p g (o u) -> p g o u", u=2)
            for c in range(CHUNKS):
                flipped = transpose_chunk(n + 1, c)
                copy_out = nc.vector.tensor_copy if c == CHUNKS - 1 else nc.scalar.copy
                copy_out(
                    out=grouped_words[:, :, c * P : (c + 1) * P, :],
                    in_=flipped[:].rearrange("p (g u) o -> p g o u", u=2),
                )
            if n + 1 + BLOCKS_AHEAD < len(blocks):
                load_block(n + 1 + BLOCKS_AHEAD)
            codes = w_mx_pool.tile([P, PASSES, F8], U32, name="w_codes", align_bytes=64)
            scales = w_mx_pool.tile([P, PASSES, F8], U8, name="w_scales", align_bytes=64)
            nc.vector.quantize_mx(
                out=codes[:].rearrange("p g o -> p (g o)").bitcast(FP8X4),
                scales=scales[:].rearrange("p g o -> p (g o)"),
                in_=grouped[:].rearrange("p g c -> p (g c)"),
            )
            w_mx[n] = (codes, scales)

        acc = {}
        gate_act = {}

        def multiply(n):
            j = n % O
            codes, scales = w_mx[n]
            for pair in range(PAIRS):
                if j == 0:
                    acc[pair] = acc_pool.tile([P, F8], F32, name="acc%d" % pair)
                for g in range(PASSES):
                    nc.tensor.matmul_mx(
                        out=acc[pair][:],
                        lhsT=x_codes[j][:, pair, g, :].bitcast(FP8X4),
                        lhsT_scale=x_scales[j][:, pair, g, :],
                        rhs=codes[:, g, :].bitcast(FP8X4),
                        rhs_scale=scales[:, g, :],
                        start=(j == 0 and g == 0),
                        stop=(j == O - 1 and g == PASSES - 1),
                    )
                if n == O - 1:
                    gate_act[pair] = keep.tile([P, F8], F32, name="gate_act%d" % pair)
                    nc.scalar.activation(
                        out=gate_act[pair][:],
                        in_=acc[pair][:],
                        func=mybir.ActivationFunctionType.Silu,
                    )
                if n == 2 * O - 1:
                    result = result_pool.tile([P, F8], F32, name="result")
                    nc.vector.tensor_tensor(
                        out=result[:], in0=acc[pair][:], in1=gate_act[pair][:], op=mybir.AluOpType.mult
                    )
                    for half in range(2):
                        nc.sync.dma_start(
                            out=out_parts[2 * pair + half],
                            in_=result[half * ROWS : (half + 1) * ROWS, :],
                        )

        quantise_x_for(0)
        prepare_w(0)
        nc.vector.tensor_scalar(
            out=x_signed[:, 1].rearrange("p i g c -> p (i g c)"),
            in0=x_signed[:, 0].rearrange("p i g c -> p (i g c)"),
            scalar1=-1.0,
            scalar2=None,
            op0=mybir.AluOpType.mult,
        )
        for n in range(1, RUN):
            quantise_x_for(n)
            prepare_w(n)
        for n in range(2 * O):
            if n % RUN == RUN - 1:
                for ahead in range(n + 1, min(n + 1 + RUN, 2 * O)):
                    if ahead < O:
                        quantise_x_for(ahead)
                    prepare_w(ahead)
            multiply(n)
